import numpy as np
import ml_dtypes

BF16 = ml_dtypes.bfloat16


def bf(x):
    return np.asarray(x, np.float32).astype(BF16)


def f32(x):
    return np.asarray(x, np.float32)


def f64(x):
    return np.asarray(x).astype(np.float64)


def striped(idx):
    return np.tile(idx.reshape(-1, 16).T, (8, 1))


CH, B, C, S, D, K, H, N = 2, 256, 512, 1024, 512, 8, 512, 4096


def setup_inputs():
    x = f32(np.random.standard_normal((C, S)))
    w = f32(np.random.standard_normal((CH, N)) * np.sqrt(2.0 / K))
    b = f32(0.1 * np.random.standard_normal((CH, D)))
    idx = np.concatenate([np.random.permutation(S)[:H] for _ in range(K)])
    return {"x": x, "w": w, "b": b, "offs": striped(idx)}


def reference(x, w, b, offs):
    idx = offs[:16].T.reshape(-1)
    prod = f64(x)[:, idx].reshape(CH, B, K, D) * f64(w).reshape(CH, 1, K, D)
    return np.maximum(prod.sum(axis=2) + f64(b).reshape(CH, 1, D), 0.0).reshape(C, D)

@@ -1,0 +1,81 @@
+import concourse.mybir as mybir
+from concourse.masks import make_identity
+
+F32 = mybir.dt.float32
+U16 = mybir.dt.uint16
+MULT = mybir.AluOpType.mult
+RELU = mybir.ActivationFunctionType.Relu
+
+P = 128
+CH = 2
+ROWS = 512
+S = 1024
+D = 512
+K = 8
+N = K * D
+BLOCKS = ROWS // P
+BLOCKS_PER_CHANNEL = BLOCKS // CH
+PIECE = S
+PIECES = N // PIECE
+NEIGHBOURS_PER_PIECE = PIECE // D
+
+FLOPS = 2 * ROWS * N
+
+
+def tile_lcnchannelstack_kernel(tc, x, w, b, offs, out):
+    nc = tc.nc
+    with (
+        tc.tile_pool(name="held", bufs=1) as held,
+        tc.tile_pool(name="products", bufs=4) as products,
+        tc.tile_pool(name="results", bufs=2) as results,
+        tc.psum_pool(name="sums", bufs=1) as sums,
+    ):
+        offsets = held.tile([P, N // 16], U16, name="offsets")
+        nc.sync.dma_start(offsets[:], offs)
+        x_block = []
+        for r in range(BLOCKS):
+            x_tile = held.tile([P, S], F32, name=f"x{r}")
+            nc.sync.dma_start(x_tile[:], x[r * P : (r + 1) * P, :])
+            x_block.append(x_tile)
+
+        w_piece = []
+        for ch in range(CH):
+            for m in range(PIECES):
+                w_tile = held.tile([P, PIECE], F32, name=f"w{ch}_{m}")
+                nc.scalar.dma_start(w_tile[:], w[ch, m * PIECE : (m + 1) * PIECE].partition_broadcast(P))
+                w_piece.append(w_tile)
+
+        bias_row = held.tile([P, CH * D], F32, name="bias_row")
+        nc.gpsimd.memset(bias_row[:], 0.0)
+        for ch in range(CH):
+            nc.gpsimd.dma_start(bias_row[0:1, ch * D : (ch + 1) * D], b[ch : ch + 1, :])
+        ones = held.tile([P, P], F32, name="ones")
+        nc.gpsimd.memset(ones[:], 1.0)
+        identity = held.tile([P, P], F32, name="identity")
+        make_identity(nc, identity[:])
+
+        total = []
+        for r in range(BLOCKS):
+            ch = r // BLOCKS_PER_CHANNEL
+            bank = sums.tile([P, D], F32, name=f"total{r}")
+            nc.tensor.matmul(bank[:], ones[:], bias_row[:, ch * D : (ch + 1) * D], start=True, stop=False)
+            total.append(bank)
+
+        for ch in range(CH):
+            blocks = range(ch * BLOCKS_PER_CHANNEL, (ch + 1) * BLOCKS_PER_CHANNEL)
+            for m in range(PIECES):
+                piece_offsets = offsets[:, m * (PIECE // 16) : (m + 1) * (PIECE // 16)]
+                for r in blocks:
+                    prod = products.tile([P, PIECE], F32, name="prod")
+                    nc.vector.tensor_tensor(
+                        prod[:], x_block[r][:].indirect(piece_offsets), w_piece[ch * PIECES + m][:], MULT
+                    )
+                    for h in range(NEIGHBOURS_PER_PIECE):
+                        k = m * NEIGHBOURS_PER_PIECE + h
+                        nc.tensor.matmul(
+                            total[r][:], identity[:], prod[:, h * D : (h + 1) * D], start=False, stop=(k == K - 1)
+                        )
+            for r in blocks:
+                result = results.tile([P, D], F32, name="result")
+                nc.scalar.activation(result[:], total[r][:], RELU)
+                nc.sync.dma_start(out[r * P : (r + 1) * P, :], result[:])

@@ -30,6 +30,13 @@ def tile_lcnchannelstack_kernel(tc, x, w, b, offs, out):
         tc.tile_pool(name="results", bufs=2) as results,
         tc.psum_pool(name="sums", bufs=1) as sums,
     ):
+        identity = held.tile([P, P], F32, name="identity")
+        make_identity(nc, identity[:])
+        ones = held.tile([P, P], F32, name="ones")
+        nc.vector.memset(ones[:], 1.0)
+        bias_row = held.tile([P, CH * D], F32, name="bias_row")
+        nc.vector.memset(bias_row[:], 0.0)
+
         offsets = held.tile([P, N // 16], U16, name="offsets")
         nc.sync.dma_start(offsets[:], offs)
         x_block = []
@@ -37,6 +44,9 @@ def tile_lcnchannelstack_kernel(tc, x, w, b, offs, out):
             x_tile = held.tile([P, S], F32, name=f"x{r}")
             nc.sync.dma_start(x_tile[:], x[r * P : (r + 1) * P, :])
             x_block.append(x_tile)
+            if r == 0:
+                for ch in range(CH):
+                    nc.sync.dma_start(bias_row[0:1, ch * D : (ch + 1) * D], b[ch : ch + 1, :])
 
         w_piece = []
         for ch in range(CH):
@@ -45,14 +55,6 @@ def tile_lcnchannelstack_kernel(tc, x, w, b, offs, out):
                 nc.scalar.dma_start(w_tile[:], w[ch, m * PIECE : (m + 1) * PIECE].partition_broadcast(P))
                 w_piece.append(w_tile)
 
-        bias_row = held.tile([P, CH * D], F32, name="bias_row")
-        nc.gpsimd.memset(bias_row[:], 0.0)
-        for ch in range(CH):
-            nc.gpsimd.dma_start(bias_row[0:1, ch * D : (ch + 1) * D], b[ch : ch + 1, :])
-        ones = held.tile([P, P], F32, name="ones")
-        nc.gpsimd.memset(ones[:], 1.0)
-        identity = held.tile([P, P], F32, name="identity")
-        make_identity(nc, identity[:])
 
         total = []
         for r in range(BLOCKS):

@@ -5,6 +5,7 @@ F32 = mybir.dt.float32
 U16 = mybir.dt.uint16
 MULT = mybir.AluOpType.mult
 RELU = mybir.ActivationFunctionType.Relu
+COPY = mybir.ActivationFunctionType.Copy
 
 P = 128
 CH = 2
@@ -15,6 +16,7 @@ K = 8
 N = K * D
 BLOCKS = ROWS // P
 BLOCKS_PER_CHANNEL = BLOCKS // CH
+QUARTERS = D // P
 PIECE = S
 PIECES = N // PIECE
 NEIGHBOURS_PER_PIECE = PIECE // D
@@ -29,13 +31,12 @@ def tile_lcnchannelstack_kernel(tc, x, w, b, offs, out):
         tc.tile_pool(name="products", bufs=4) as products,
         tc.tile_pool(name="results", bufs=2) as results,
         tc.psum_pool(name="sums", bufs=1) as sums,
+        tc.psum_pool(name="backs", bufs=2) as backs,
     ):
         identity = held.tile([P, P], F32, name="identity")
         make_identity(nc, identity[:])
-        ones = held.tile([P, P], F32, name="ones")
-        nc.vector.memset(ones[:], 1.0)
-        bias_row = held.tile([P, CH * D], F32, name="bias_row")
-        nc.vector.memset(bias_row[:], 0.0)
+        b_rows = held.tile([P, P], F32, name="b_rows")
+        nc.vector.memset(b_rows[:], 0.0)
 
         offsets = held.tile([P, N // 16], U16, name="offsets")
         nc.sync.dma_start(offsets[:], offs)
@@ -45,8 +46,7 @@ def tile_lcnchannelstack_kernel(tc, x, w, b, offs, out):
             nc.sync.dma_start(x_tile[:], x[r * P : (r + 1) * P, :])
             x_block.append(x_tile)
             if r == 0:
-                for ch in range(CH):
-                    nc.sync.dma_start(bias_row[0:1, ch * D : (ch + 1) * D], b[ch : ch + 1, :])
+                nc.sync.dma_start(b_rows[0 : CH * QUARTERS, :], b.rearrange("c (q p) -> (c q) p", p=P))
 
         w_piece = []
         for ch in range(CH):
@@ -55,13 +55,12 @@ def tile_lcnchannelstack_kernel(tc, x, w, b, offs, out):
                 nc.scalar.dma_start(w_tile[:], w[ch, m * PIECE : (m + 1) * PIECE].partition_broadcast(P))
                 w_piece.append(w_tile)
 
+        b_flipped = sums.tile([P, P], F32, name="b_flipped")
+        nc.tensor.transpose(b_flipped[:], b_rows[:], identity[:])
+        bias = held.tile([P, CH * QUARTERS], F32, name="bias")
+        nc.scalar.activation(bias[:], b_flipped[:, 0 : CH * QUARTERS], COPY)
 
-        total = []
-        for r in range(BLOCKS):
-            ch = r // BLOCKS_PER_CHANNEL
-            bank = sums.tile([P, D], F32, name=f"total{r}")
-            nc.tensor.matmul(bank[:], ones[:], bias_row[:, ch * D : (ch + 1) * D], start=True, stop=False)
-            total.append(bank)
+        total = [sums.tile([P, D], F32, name=f"total{r}") for r in range(BLOCKS)]
 
         for ch in range(CH):
             blocks = range(ch * BLOCKS_PER_CHANNEL, (ch + 1) * BLOCKS_PER_CHANNEL)
@@ -74,10 +73,24 @@ def tile_lcnchannelstack_kernel(tc, x, w, b, offs, out):
                     )
                     for h in range(NEIGHBOURS_PER_PIECE):
                         k = m * NEIGHBOURS_PER_PIECE + h
-                        nc.tensor.matmul(
-                            total[r][:], identity[:], prod[:, h * D : (h + 1) * D], start=False, stop=(k == K - 1)
-                        )
+                        for q in range(QUARTERS):
+                            nc.tensor.matmul(
+                                total[r][:, q * P : (q + 1) * P],
+                                prod[:, h * D + q * P : h * D + (q + 1) * P],
+                                identity[:],
+                                is_transpose=True,
+                                start=(k == 0 and q == 0),
+                                stop=(k == K - 1 and q == QUARTERS - 1),
+                            )
             for r in blocks:
+                flipped = results.tile([P, D], F32, name="flipped")
+                back = backs.tile([P, D], F32, name="back")
+                for q in range(QUARTERS):
+                    square = slice(q * P, (q + 1) * P)
+                    nc.scalar.activation(
+                        flipped[:, square], total[r][:, square], RELU, bias=bias[:, ch * QUARTERS + q : ch * QUARTERS + q + 1]
+                    )
+                    nc.tensor.transpose(back[:, square], flipped[:, square], identity[:])
                 result = results.tile([P, D], F32, name="result")
-                nc.scalar.activation(result[:], total[r][:], RELU)
+                nc.scalar.activation(result[:], back[:], COPY)
                 nc.sync.dma_start(out[r * P : (r + 1) * P, :], result[:])

@@ -14,12 +14,11 @@ S = 1024
 D = 512
 K = 8
 N = K * D
-BLOCKS = ROWS // P
-BLOCKS_PER_CHANNEL = BLOCKS // CH
-QUARTERS = D // P
-PIECE = S
+BLOCKS_PER_CHANNEL = ROWS // P // CH
+SQUARES = D // P
+NEIGHBOURS_PER_PIECE = 2
+PIECE = NEIGHBOURS_PER_PIECE * D
 PIECES = N // PIECE
-NEIGHBOURS_PER_PIECE = PIECE // D
 
 FLOPS = 2 * ROWS * N
 
@@ -30,23 +29,24 @@ def tile_lcnchannelstack_kernel(tc, x, w, b, offs, out):
         tc.tile_pool(name="held", bufs=1) as held,
         tc.tile_pool(name="products", bufs=4) as products,
         tc.tile_pool(name="results", bufs=2) as results,
-        tc.psum_pool(name="sums", bufs=1) as sums,
+        tc.psum_pool(name="totals", bufs=1) as totals,
         tc.psum_pool(name="backs", bufs=2) as backs,
     ):
         identity = held.tile([P, P], F32, name="identity")
         make_identity(nc, identity[:])
-        b_rows = held.tile([P, P], F32, name="b_rows")
-        nc.vector.memset(b_rows[:], 0.0)
 
         offsets = held.tile([P, N // 16], U16, name="offsets")
         nc.sync.dma_start(offsets[:], offs)
         x_block = []
-        for r in range(BLOCKS):
-            x_tile = held.tile([P, S], F32, name=f"x{r}")
-            nc.sync.dma_start(x_tile[:], x[r * P : (r + 1) * P, :])
-            x_block.append(x_tile)
-            if r == 0:
-                nc.sync.dma_start(b_rows[0 : CH * QUARTERS, :], b.rearrange("c (q p) -> (c q) p", p=P))
+        bias = []
+        for ch in range(CH):
+            for r in range(ch * BLOCKS_PER_CHANNEL, (ch + 1) * BLOCKS_PER_CHANNEL):
+                x_tile = held.tile([P, S], F32, name=f"x{r}")
+                nc.sync.dma_start(x_tile[:], x[r * P : (r + 1) * P, :])
+                x_block.append(x_tile)
+            b_tile = held.tile([P, D], F32, name=f"b{ch}")
+            nc.sync.dma_start(b_tile[:], b[ch, :].partition_broadcast(P))
+            bias.append(b_tile)
 
         w_piece = []
         for ch in range(CH):
@@ -55,15 +55,24 @@ def tile_lcnchannelstack_kernel(tc, x, w, b, offs, out):
                 nc.scalar.dma_start(w_tile[:], w[ch, m * PIECE : (m + 1) * PIECE].partition_broadcast(P))
                 w_piece.append(w_tile)
 
-        b_flipped = sums.tile([P, P], F32, name="b_flipped")
-        nc.tensor.transpose(b_flipped[:], b_rows[:], identity[:])
-        bias = held.tile([P, CH * QUARTERS], F32, name="bias")
-        nc.scalar.activation(bias[:], b_flipped[:, 0 : CH * QUARTERS], COPY)
-
-        total = [sums.tile([P, D], F32, name=f"total{r}") for r in range(BLOCKS)]
+        def add_flipped(total, term, first, last):
+            for q in range(SQUARES):
+                nc.tensor.matmul(
+                    total[:, q * P : (q + 1) * P],
+                    term[:, q * P : (q + 1) * P],
+                    identity[:],
+                    is_transpose=True,
+                    start=(first and q == 0),
+                    stop=(last and q == SQUARES - 1),
+                )
 
         for ch in range(CH):
             blocks = range(ch * BLOCKS_PER_CHANNEL, (ch + 1) * BLOCKS_PER_CHANNEL)
+            total = {}
+            for r in blocks:
+                total[r] = totals.tile([P, D], F32, name=f"total{r}")
+                add_flipped(total[r], bias[ch], first=True, last=False)
+
             for m in range(PIECES):
                 piece_offsets = offsets[:, m * (PIECE // 16) : (m + 1) * (PIECE // 16)]
                 for r in blocks:
@@ -73,24 +82,14 @@ def tile_lcnchannelstack_kernel(tc, x, w, b, offs, out):
                     )
                     for h in range(NEIGHBOURS_PER_PIECE):
                         k = m * NEIGHBOURS_PER_PIECE + h
-                        for q in range(QUARTERS):
-                            nc.tensor.matmul(
-                                total[r][:, q * P : (q + 1) * P],
-                                prod[:, h * D + q * P : h * D + (q + 1) * P],
-                                identity[:],
-                                is_transpose=True,
-                                start=(k == 0 and q == 0),
-                                stop=(k == K - 1 and q == QUARTERS - 1),
-                            )
+                        add_flipped(total[r], prod[:, h * D : (h + 1) * D], first=False, last=(k == K - 1))
+
             for r in blocks:
                 flipped = results.tile([P, D], F32, name="flipped")
+                nc.scalar.activation(flipped[:], total[r][:], RELU)
                 back = backs.tile([P, D], F32, name="back")
-                for q in range(QUARTERS):
-                    square = slice(q * P, (q + 1) * P)
-                    nc.scalar.activation(
-                        flipped[:, square], total[r][:, square], RELU, bias=bias[:, ch * QUARTERS + q : ch * QUARTERS + q + 1]
-                    )
-                    nc.tensor.transpose(back[:, square], flipped[:, square], identity[:])
+                for q in range(SQUARES):
+                    nc.tensor.transpose(back[:, q * P : (q + 1) * P], flipped[:, q * P : (q + 1) * P], identity[:])
                 result = results.tile([P, D], F32, name="result")
                 nc.scalar.activation(result[:], back[:], COPY)
                 nc.sync.dma_start(out[r * P : (r + 1) * P, :], result[:])

@@ -4,6 +4,7 @@ from concourse.masks import make_identity
 F32 = mybir.dt.float32
 U16 = mybir.dt.uint16
 MULT = mybir.AluOpType.mult
+ADD = mybir.AluOpType.add
 RELU = mybir.ActivationFunctionType.Relu
 COPY = mybir.ActivationFunctionType.Copy
 
@@ -14,7 +15,8 @@ S = 1024
 D = 512
 K = 8
 N = K * D
-BLOCKS_PER_CHANNEL = ROWS // P // CH
+BLOCKS = ROWS // P
+BLOCKS_PER_CHANNEL = BLOCKS // CH
 SQUARES = D // P
 NEIGHBOURS_PER_PIECE = 2
 PIECE = NEIGHBOURS_PER_PIECE * D
@@ -29,7 +31,7 @@ def tile_lcnchannelstack_kernel(tc, x, w, b, offs, out):
         tc.tile_pool(name="held", bufs=1) as held,
         tc.tile_pool(name="products", bufs=4) as products,
         tc.tile_pool(name="results", bufs=2) as results,
-        tc.psum_pool(name="totals", bufs=1) as totals,
+        tc.psum_pool(name="totals", bufs=2) as totals,
         tc.psum_pool(name="backs", bufs=2) as backs,
     ):
         identity = held.tile([P, P], F32, name="identity")
@@ -66,30 +68,55 @@ def tile_lcnchannelstack_kernel(tc, x, w, b, offs, out):
                     stop=(last and q == SQUARES - 1),
                 )
 
-        for ch in range(CH):
-            blocks = range(ch * BLOCKS_PER_CHANNEL, (ch + 1) * BLOCKS_PER_CHANNEL)
-            total = {}
-            for r in blocks:
-                total[r] = totals.tile([P, D], F32, name=f"total{r}")
-                add_flipped(total[r], bias[ch], first=True, last=False)
+        def flip_back(flipped):
+            back = backs.tile([P, D], F32, name="back")
+            for q in range(SQUARES):
+                nc.tensor.transpose(back[:, q * P : (q + 1) * P], flipped[:, q * P : (q + 1) * P], identity[:])
+            return back
 
+        def look_up(r, first_entry, entries):
+            ch = r // BLOCKS_PER_CHANNEL
+            m, start = divmod(first_entry, PIECE)
+            prod = products.tile([P, entries], F32, name="prod")
+            nc.vector.tensor_tensor(
+                prod[:],
+                x_block[r][:].indirect(offsets[:, first_entry // 16 : (first_entry + entries) // 16]),
+                w_piece[ch * PIECES + m][:, start : start + entries],
+                MULT,
+            )
+            return prod
+
+        for r in range(BLOCKS - 1):
+            total = totals.tile([P, D], F32, name="total")
+            add_flipped(total, bias[r // BLOCKS_PER_CHANNEL], first=True, last=False)
             for m in range(PIECES):
-                piece_offsets = offsets[:, m * (PIECE // 16) : (m + 1) * (PIECE // 16)]
-                for r in blocks:
-                    prod = products.tile([P, PIECE], F32, name="prod")
-                    nc.vector.tensor_tensor(
-                        prod[:], x_block[r][:].indirect(piece_offsets), w_piece[ch * PIECES + m][:], MULT
-                    )
-                    for h in range(NEIGHBOURS_PER_PIECE):
-                        k = m * NEIGHBOURS_PER_PIECE + h
-                        add_flipped(total[r], prod[:, h * D : (h + 1) * D], first=False, last=(k == K - 1))
+                prod = look_up(r, m * PIECE, PIECE)
+                for h in range(NEIGHBOURS_PER_PIECE):
+                    k = m * NEIGHBOURS_PER_PIECE + h
+                    add_flipped(total, prod[:, h * D : (h + 1) * D], first=False, last=(k == K - 1))
+            flipped = results.tile([P, D], F32, name="flipped")
+            nc.scalar.activation(flipped[:], total[:], RELU)
+            back = flip_back(flipped)
+            result = results.tile([P, D], F32, name="result")
+            nc.scalar.activation(result[:], back[:], COPY)
+            nc.sync.dma_start(out[r * P : (r + 1) * P, :], result[:])
 
-            for r in blocks:
-                flipped = results.tile([P, D], F32, name="flipped")
-                nc.scalar.activation(flipped[:], total[r][:], RELU)
-                back = backs.tile([P, D], F32, name="back")
-                for q in range(SQUARES):
-                    nc.tensor.transpose(back[:, q * P : (q + 1) * P], flipped[:, q * P : (q + 1) * P], identity[:])
-                result = results.tile([P, D], F32, name="result")
-                nc.scalar.activation(result[:], back[:], COPY)
-                nc.sync.dma_start(out[r * P : (r + 1) * P, :], result[:])
+        r = BLOCKS - 1
+        total = totals.tile([P, D], F32, name="total")
+        add_flipped(total, bias[r // BLOCKS_PER_CHANNEL], first=True, last=False)
+        for m in range(PIECES - 1):
+            prod = look_up(r, m * PIECE, PIECE)
+            for h in range(NEIGHBOURS_PER_PIECE):
+                last = m == PIECES - 2 and h == NEIGHBOURS_PER_PIECE - 1
+                add_flipped(total, prod[:, h * D : (h + 1) * D], first=False, last=last)
+        flipped = results.tile([P, D], F32, name="flipped")
+        nc.scalar.activation(flipped[:], total[:], COPY)
+        back = flip_back(flipped)
+        prod = look_up(r, (PIECES - 1) * PIECE, PIECE)
+        pair = results.tile([P, D], F32, name="pair")
+        nc.vector.tensor_tensor(pair[:], prod[:, 0:D], prod[:, D : 2 * D], ADD)
+        summed = results.tile([P, D], F32, name="summed")
+        nc.vector.tensor_tensor(summed[:], pair[:], back[:], ADD)
+        result = results.tile([P, D], F32, name="result")
+        nc.vector.tensor_scalar_max(result[:], summed[:], 0.0)
+        nc.sync.dma_start(out[r * P : (r + 1) * P, :], result[:])

@@ -21,6 +21,7 @@ SQUARES = D // P
 NEIGHBOURS_PER_PIECE = 2
 PIECE = NEIGHBOURS_PER_PIECE * D
 PIECES = N // PIECE
+FIRST_LOOK_UP = 256
 
 FLOPS = 2 * ROWS * N
 
@@ -40,32 +41,38 @@ def tile_lcnchannelstack_kernel(tc, x, w, b, offs, out):
         offsets = held.tile([P, N // 16], U16, name="offsets")
         nc.sync.dma_start(offsets[:], offs)
         x_block = []
-        bias = []
-        for ch in range(CH):
-            for r in range(ch * BLOCKS_PER_CHANNEL, (ch + 1) * BLOCKS_PER_CHANNEL):
-                x_tile = held.tile([P, S], F32, name=f"x{r}")
-                nc.sync.dma_start(x_tile[:], x[r * P : (r + 1) * P, :])
-                x_block.append(x_tile)
-            b_tile = held.tile([P, D], F32, name=f"b{ch}")
-            nc.sync.dma_start(b_tile[:], b[ch, :].partition_broadcast(P))
-            bias.append(b_tile)
-
         w_piece = []
-        for ch in range(CH):
-            for m in range(PIECES):
-                w_tile = held.tile([P, PIECE], F32, name=f"w{ch}_{m}")
-                nc.scalar.dma_start(w_tile[:], w[ch, m * PIECE : (m + 1) * PIECE].partition_broadcast(P))
-                w_piece.append(w_tile)
+        bias = []
+        for r in range(BLOCKS):
+            x_tile = held.tile([P, S], F32, name=f"x{r}")
+            nc.sync.dma_start(x_tile[:], x[r * P : (r + 1) * P, :])
+            x_block.append(x_tile)
+            if r % BLOCKS_PER_CHANNEL == 0:
+                ch = r // BLOCKS_PER_CHANNEL
+                for m in range(PIECES):
+                    w_tile = held.tile([P, PIECE], F32, name=f"w{ch}_{m}")
+                    cuts = [0, FIRST_LOOK_UP, PIECE] if r == 0 and m == 0 else [0, PIECE]
+                    for lo, hi in zip(cuts[:-1], cuts[1:]):
+                        nc.sync.dma_start(
+                            w_tile[:, lo:hi], w[ch, m * PIECE + lo : m * PIECE + hi].partition_broadcast(P)
+                        )
+                    w_piece.append(w_tile)
+                    if m == 0:
+                        b_tile = held.tile([P, D], F32, name=f"b{ch}")
+                        nc.sync.dma_start(b_tile[:], b[ch, :].partition_broadcast(P))
+                        bias.append(b_tile)
 
-        def add_flipped(total, term, first, last):
-            for q in range(SQUARES):
+        def add_flipped(total, term, first_entry, entries, first=False, last=False):
+            squares = entries // P
+            for s in range(squares):
+                q = (first_entry // P + s) % SQUARES
                 nc.tensor.matmul(
                     total[:, q * P : (q + 1) * P],
-                    term[:, q * P : (q + 1) * P],
+                    term[:, s * P : (s + 1) * P],
                     identity[:],
                     is_transpose=True,
-                    start=(first and q == 0),
-                    stop=(last and q == SQUARES - 1),
+                    start=(first and s == 0),
+                    stop=(last and s == squares - 1),
                 )
 
         def flip_back(flipped):
@@ -88,12 +95,12 @@ def tile_lcnchannelstack_kernel(tc, x, w, b, offs, out):
 
         for r in range(BLOCKS - 1):
             total = totals.tile([P, D], F32, name="total")
-            add_flipped(total, bias[r // BLOCKS_PER_CHANNEL], first=True, last=False)
-            for m in range(PIECES):
-                prod = look_up(r, m * PIECE, PIECE)
-                for h in range(NEIGHBOURS_PER_PIECE):
-                    k = m * NEIGHBOURS_PER_PIECE + h
-                    add_flipped(total, prod[:, h * D : (h + 1) * D], first=False, last=(k == K - 1))
+            add_flipped(total, bias[r // BLOCKS_PER_CHANNEL], 0, D, first=True)
+            cuts = [0, FIRST_LOOK_UP] if r == 0 else [0]
+            cuts = cuts + [m * PIECE for m in range(1, PIECES + 1)]
+            for lo, hi in zip(cuts[:-1], cuts[1:]):
+                prod = look_up(r, lo, hi - lo)
+                add_flipped(total, prod, lo, hi - lo, last=(hi == N))
             flipped = results.tile([P, D], F32, name="flipped")
             nc.scalar.activation(flipped[:], total[:], RELU)
             back = flip_back(flipped)
@@ -103,12 +110,10 @@ def tile_lcnchannelstack_kernel(tc, x, w, b, offs, out):
 
         r = BLOCKS - 1
         total = totals.tile([P, D], F32, name="total")
-        add_flipped(total, bias[r // BLOCKS_PER_CHANNEL], first=True, last=False)
+        add_flipped(total, bias[r // BLOCKS_PER_CHANNEL], 0, D, first=True)
         for m in range(PIECES - 1):
             prod = look_up(r, m * PIECE, PIECE)
-            for h in range(NEIGHBOURS_PER_PIECE):
-                last = m == PIECES - 2 and h == NEIGHBOURS_PER_PIECE - 1
-                add_flipped(total, prod[:, h * D : (h + 1) * D], first=False, last=last)
+            add_flipped(total, prod, m * PIECE, PIECE, last=(m == PIECES - 2))
         flipped = results.tile([P, D], F32, name="flipped")
         nc.scalar.activation(flipped[:], total[:], COPY)
         back = flip_back(flipped)

@@ -22,6 +22,7 @@ NEIGHBOURS_PER_PIECE = 2
 PIECE = NEIGHBOURS_PER_PIECE * D
 PIECES = N // PIECE
 FIRST_LOOK_UP = 256
+HALF = D // 2
 
 FLOPS = 2 * ROWS * N
 
@@ -32,7 +33,7 @@ def tile_lcnchannelstack_kernel(tc, x, w, b, offs, out):
         tc.tile_pool(name="held", bufs=1) as held,
         tc.tile_pool(name="products", bufs=4) as products,
         tc.tile_pool(name="results", bufs=2) as results,
-        tc.psum_pool(name="totals", bufs=2) as totals,
+        tc.psum_pool(name="totals", bufs=3) as totals,
         tc.psum_pool(name="backs", bufs=2) as backs,
     ):
         identity = held.tile([P, P], F32, name="identity")
@@ -62,22 +63,32 @@ def tile_lcnchannelstack_kernel(tc, x, w, b, offs, out):
                         nc.sync.dma_start(b_tile[:], b[ch, :].partition_broadcast(P))
                         bias.append(b_tile)
 
-        def add_flipped(total, term, first_entry, entries, first=False, last=False):
-            squares = entries // P
-            for s in range(squares):
-                q = (first_entry // P + s) % SQUARES
+        def open_sums(parts, terms):
+            return [
+                {"bank": totals.tile([P, D // parts], F32, name="total"), "done": 0, "squares": terms * SQUARES // parts}
+                for part in range(parts)
+            ]
+
+        def add_flipped(sums, term, first_entry, entries):
+            squares_per_bank = SQUARES // len(sums)
+            for s in range(entries // P):
+                part, q = divmod((first_entry // P + s) % SQUARES, squares_per_bank)
+                group = sums[part]
+                group["done"] += 1
                 nc.tensor.matmul(
-                    total[:, q * P : (q + 1) * P],
+                    group["bank"][:, q * P : (q + 1) * P],
                     term[:, s * P : (s + 1) * P],
                     identity[:],
                     is_transpose=True,
-                    start=(first and s == 0),
-                    stop=(last and s == squares - 1),
+                    start=(group["done"] == 1),
+                    stop=(group["done"] == group["squares"]),
                 )
 
-        def flip_back(flipped):
-            back = backs.tile([P, D], F32, name="back")
-            for q in range(SQUARES):
+        def flip_back(bank, columns, func):
+            flipped = results.tile([P, columns], F32, name="flipped")
+            nc.scalar.activation(flipped[:], bank[:], func)
+            back = backs.tile([P, columns], F32, name="back")
+            for q in range(columns // P):
                 nc.tensor.transpose(back[:, q * P : (q + 1) * P], flipped[:, q * P : (q + 1) * P], identity[:])
             return back
 
@@ -94,34 +105,38 @@ def tile_lcnchannelstack_kernel(tc, x, w, b, offs, out):
             return prod
 
         for r in range(BLOCKS - 1):
-            total = totals.tile([P, D], F32, name="total")
-            add_flipped(total, bias[r // BLOCKS_PER_CHANNEL], 0, D, first=True)
+            sums = open_sums(parts=1, terms=1 + K)
+            add_flipped(sums, bias[r // BLOCKS_PER_CHANNEL], 0, D)
             cuts = [0, FIRST_LOOK_UP] if r == 0 else [0]
             cuts = cuts + [m * PIECE for m in range(1, PIECES + 1)]
             for lo, hi in zip(cuts[:-1], cuts[1:]):
-                prod = look_up(r, lo, hi - lo)
-                add_flipped(total, prod, lo, hi - lo, last=(hi == N))
-            flipped = results.tile([P, D], F32, name="flipped")
-            nc.scalar.activation(flipped[:], total[:], RELU)
-            back = flip_back(flipped)
+                add_flipped(sums, look_up(r, lo, hi - lo), lo, hi - lo)
+            back = flip_back(sums[0]["bank"], D, RELU)
             result = results.tile([P, D], F32, name="result")
             nc.scalar.activation(result[:], back[:], COPY)
             nc.sync.dma_start(out[r * P : (r + 1) * P, :], result[:])
 
         r = BLOCKS - 1
-        total = totals.tile([P, D], F32, name="total")
-        add_flipped(total, bias[r // BLOCKS_PER_CHANNEL], 0, D, first=True)
+        rows = out[r * P : (r + 1) * P, :]
+        left, right = open_sums(parts=2, terms=1 + K)
+        right["squares"] -= NEIGHBOURS_PER_PIECE * HALF // P
+        add_flipped([left, right], bias[r // BLOCKS_PER_CHANNEL], 0, D)
         for m in range(PIECES - 1):
-            prod = look_up(r, m * PIECE, PIECE)
-            add_flipped(total, prod, m * PIECE, PIECE, last=(m == PIECES - 2))
-        flipped = results.tile([P, D], F32, name="flipped")
-        nc.scalar.activation(flipped[:], total[:], COPY)
-        back = flip_back(flipped)
-        prod = look_up(r, (PIECES - 1) * PIECE, PIECE)
-        pair = results.tile([P, D], F32, name="pair")
-        nc.vector.tensor_tensor(pair[:], prod[:, 0:D], prod[:, D : 2 * D], ADD)
-        summed = results.tile([P, D], F32, name="summed")
-        nc.vector.tensor_tensor(summed[:], pair[:], back[:], ADD)
-        result = results.tile([P, D], F32, name="result")
-        nc.vector.tensor_scalar_max(result[:], summed[:], 0.0)
-        nc.sync.dma_start(out[r * P : (r + 1) * P, :], result[:])
+            add_flipped([left, right], look_up(r, m * PIECE, PIECE), m * PIECE, PIECE)
+        for k in (K - 2, K - 1):
+            add_flipped([left, right], look_up(r, k * D, HALF), k * D, HALF)
+        right_prod = [look_up(r, k * D + HALF, HALF) for k in (K - 2, K - 1)]
+
+        right_back = flip_back(right["bank"], HALF, COPY)
+        left_back = flip_back(left["bank"], HALF, RELU)
+        left_result = results.tile([P, HALF], F32, name="left_result")
+        nc.scalar.activation(left_result[:], left_back[:], COPY)
+        nc.sync.dma_start(rows[:, 0:HALF], left_result[:])
+
+        pair = results.tile([P, HALF], F32, name="pair")
+        nc.vector.tensor_tensor(pair[:], right_prod[0][:], right_prod[1][:], ADD)
+        summed = results.tile([P, HALF], F32, name="summed")
+        nc.vector.tensor_tensor(summed[:], pair[:], right_back[:], ADD)
+        right_result = results.tile([P, HALF], F32, name="right_result")
+        nc.vector.tensor_scalar_max(right_result[:], summed[:], 0.0)
+        nc.sync.dma_start(rows[:, HALF:D], right_result[:])

@@ -133,10 +133,10 @@ def tile_lcnchannelstack_kernel(tc, x, w, b, offs, out):
         nc.scalar.activation(left_result[:], left_back[:], COPY)
         nc.sync.dma_start(rows[:, 0:HALF], left_result[:])
 
-        pair = results.tile([P, HALF], F32, name="pair")
-        nc.vector.tensor_tensor(pair[:], right_prod[0][:], right_prod[1][:], ADD)
+        all_but_last = results.tile([P, HALF], F32, name="all_but_last")
+        nc.vector.tensor_tensor(all_but_last[:], right_prod[0][:], right_back[:], ADD)
         summed = results.tile([P, HALF], F32, name="summed")
-        nc.vector.tensor_tensor(summed[:], pair[:], right_back[:], ADD)
+        nc.vector.tensor_tensor(summed[:], right_prod[1][:], all_but_last[:], ADD)
         right_result = results.tile([P, HALF], F32, name="right_result")
         nc.vector.tensor_scalar_max(right_result[:], summed[:], 0.0)
         nc.sync.dma_start(rows[:, HALF:D], right_result[:])

@@ -40,28 +40,35 @@ def tile_lcnchannelstack_kernel(tc, x, w, b, offs, out):
         make_identity(nc, identity[:])
 
         offsets = held.tile([P, N // 16], U16, name="offsets")
+        x_block = [held.tile([P, S], F32, name=f"x{r}") for r in range(BLOCKS)]
+        w_piece = [held.tile([P, PIECE], F32, name=f"w{i}") for i in range(CH * PIECES)]
+        bias = [held.tile([P, D], F32, name=f"b{ch}") for ch in range(CH)]
+
+        def load_x(r):
+            nc.sync.dma_start(x_block[r][:], x[r * P : (r + 1) * P, :])
+
+        def load_w(ch, m, lo=0, hi=PIECE):
+            nc.sync.dma_start(
+                w_piece[ch * PIECES + m][:, lo:hi], w[ch, m * PIECE + lo : m * PIECE + hi].partition_broadcast(P)
+            )
+
+        def load_b(ch):
+            nc.sync.dma_start(bias[ch][:], b[ch, :].partition_broadcast(P))
+
         nc.sync.dma_start(offsets[:], offs)
-        x_block = []
-        w_piece = []
-        bias = []
-        for r in range(BLOCKS):
-            x_tile = held.tile([P, S], F32, name=f"x{r}")
-            nc.sync.dma_start(x_tile[:], x[r * P : (r + 1) * P, :])
-            x_block.append(x_tile)
-            if r % BLOCKS_PER_CHANNEL == 0:
-                ch = r // BLOCKS_PER_CHANNEL
-                for m in range(PIECES):
-                    w_tile = held.tile([P, PIECE], F32, name=f"w{ch}_{m}")
-                    cuts = [0, FIRST_LOOK_UP, PIECE] if r == 0 and m == 0 else [0, PIECE]
-                    for lo, hi in zip(cuts[:-1], cuts[1:]):
-                        nc.sync.dma_start(
-                            w_tile[:, lo:hi], w[ch, m * PIECE + lo : m * PIECE + hi].partition_broadcast(P)
-                        )
-                    w_piece.append(w_tile)
-                    if m == 0:
-                        b_tile = held.tile([P, D], F32, name=f"b{ch}")
-                        nc.sync.dma_start(b_tile[:], b[ch, :].partition_broadcast(P))
-                        bias.append(b_tile)
+        load_w(0, 0, 0, FIRST_LOOK_UP)
+        load_x(0)
+        load_w(0, 0, FIRST_LOOK_UP, PIECE)
+        load_b(0)
+        for m in range(1, PIECES):
+            load_w(0, m)
+        load_x(1)
+        load_x(2)
+        load_w(1, 0)
+        load_b(1)
+        for m in range(1, PIECES):
+            load_w(1, m)
+        load_x(3)
 
         def open_sums(parts, terms):
             return [

@@ -21,7 +21,7 @@ SQUARES = D // P
 NEIGHBOURS_PER_PIECE = 2
 PIECE = NEIGHBOURS_PER_PIECE * D
 PIECES = N // PIECE
-FIRST_LOOK_UP = 256
+FIRST_CUTS = [0, 128, 512, 1024]
 HALF = D // 2
 
 FLOPS = 2 * ROWS * N
@@ -56,9 +56,10 @@ def tile_lcnchannelstack_kernel(tc, x, w, b, offs, out):
             nc.sync.dma_start(bias[ch][:], b[ch, :].partition_broadcast(P))
 
         nc.sync.dma_start(offsets[:], offs)
-        load_w(0, 0, 0, FIRST_LOOK_UP)
+        load_w(0, 0, FIRST_CUTS[0], FIRST_CUTS[1])
         load_x(0)
-        load_w(0, 0, FIRST_LOOK_UP, PIECE)
+        for lo, hi in zip(FIRST_CUTS[1:-1], FIRST_CUTS[2:]):
+            load_w(0, 0, lo, hi)
         load_b(0)
         for m in range(1, PIECES):
             load_w(0, m)
@@ -114,8 +115,8 @@ def tile_lcnchannelstack_kernel(tc, x, w, b, offs, out):
         for r in range(BLOCKS - 1):
             sums = open_sums(parts=1, terms=1 + K)
             add_flipped(sums, bias[r // BLOCKS_PER_CHANNEL], 0, D)
-            cuts = [0, FIRST_LOOK_UP] if r == 0 else [0]
-            cuts = cuts + [m * PIECE for m in range(1, PIECES + 1)]
+            cuts = FIRST_CUTS if r == 0 else [0, PIECE]
+            cuts = cuts + [m * PIECE for m in range(2, PIECES + 1)]
             for lo, hi in zip(cuts[:-1], cuts[1:]):
                 add_flipped(sums, look_up(r, lo, hi - lo), lo, hi - lo)
             back = flip_back(sums[0]["bank"], D, RELU)

@@ -60,15 +60,14 @@ def tile_lcnchannelstack_kernel(tc, x, w, b, offs, out):
         load_x(0)
         for lo, hi in zip(FIRST_CUTS[1:-1], FIRST_CUTS[2:]):
             load_w(0, 0, lo, hi)
-        load_b(0)
         for m in range(1, PIECES):
             load_w(0, m)
+        load_b(0)
         load_x(1)
         load_x(2)
-        load_w(1, 0)
-        load_b(1)
-        for m in range(1, PIECES):
+        for m in range(PIECES):
             load_w(1, m)
+        load_b(1)
         load_x(3)
 
         def open_sums(parts, terms):
@@ -113,12 +112,12 @@ def tile_lcnchannelstack_kernel(tc, x, w, b, offs, out):
             return prod
 
         for r in range(BLOCKS - 1):
-            sums = open_sums(parts=1, terms=1 + K)
-            add_flipped(sums, bias[r // BLOCKS_PER_CHANNEL], 0, D)
+            sums = open_sums(parts=1, terms=K + 1)
             cuts = FIRST_CUTS if r == 0 else [0, PIECE]
             cuts = cuts + [m * PIECE for m in range(2, PIECES + 1)]
             for lo, hi in zip(cuts[:-1], cuts[1:]):
                 add_flipped(sums, look_up(r, lo, hi - lo), lo, hi - lo)
+            add_flipped(sums, bias[r // BLOCKS_PER_CHANNEL], 0, D)
             back = flip_back(sums[0]["bank"], D, RELU)
             result = results.tile([P, D], F32, name="result")
             nc.scalar.activation(result[:], back[:], COPY)

@@ -23,6 +23,7 @@ PIECE = NEIGHBOURS_PER_PIECE * D
 PIECES = N // PIECE
 FIRST_CUTS = [0, 128, 512, 1024]
 HALF = D // 2
+HALF_SQUARES = HALF // P
 
 FLOPS = 2 * ROWS * N
 
@@ -70,26 +71,27 @@ def tile_lcnchannelstack_kernel(tc, x, w, b, offs, out):
         load_b(1)
         load_x(3)
 
-        def open_sums(parts, terms):
-            return [
-                {"bank": totals.tile([P, D // parts], F32, name="total"), "done": 0, "squares": terms * SQUARES // parts}
-                for part in range(parts)
-            ]
+        def open_sum(columns, matmuls):
+            return {"bank": totals.tile([P, columns], F32, name="total"), "done": 0, "matmuls": matmuls}
 
-        def add_flipped(sums, term, first_entry, entries):
-            squares_per_bank = SQUARES // len(sums)
-            for s in range(entries // P):
-                part, q = divmod((first_entry // P + s) % SQUARES, squares_per_bank)
-                group = sums[part]
-                group["done"] += 1
+        def group_flags(group):
+            group["done"] += 1
+            return {"start": group["done"] == 1, "stop": group["done"] == group["matmuls"]}
+
+        def add_flipped(group, term, first_square=0):
+            squares = group["bank"][:].shape[1] // P
+            for s in range(term.shape[1] // P):
+                q = (first_square + s) % squares
                 nc.tensor.matmul(
                     group["bank"][:, q * P : (q + 1) * P],
                     term[:, s * P : (s + 1) * P],
                     identity[:],
                     is_transpose=True,
-                    start=(group["done"] == 1),
-                    stop=(group["done"] == group["squares"]),
+                    **group_flags(group),
                 )
+
+        def add_plain(group, term):
+            nc.tensor.matmul(group["bank"][:], identity[:], term, **group_flags(group))
 
         def flip_back(bank, columns, func):
             flipped = results.tile([P, columns], F32, name="flipped")
@@ -112,38 +114,47 @@ def tile_lcnchannelstack_kernel(tc, x, w, b, offs, out):
             return prod
 
         for r in range(BLOCKS - 1):
-            sums = open_sums(parts=1, terms=K + 1)
+            total = open_sum(D, (K + 1) * SQUARES)
             cuts = FIRST_CUTS if r == 0 else [0, PIECE]
             cuts = cuts + [m * PIECE for m in range(2, PIECES + 1)]
             for lo, hi in zip(cuts[:-1], cuts[1:]):
-                add_flipped(sums, look_up(r, lo, hi - lo), lo, hi - lo)
-            add_flipped(sums, bias[r // BLOCKS_PER_CHANNEL], 0, D)
-            back = flip_back(sums[0]["bank"], D, RELU)
+                add_flipped(total, look_up(r, lo, hi - lo)[:], lo // P)
+            add_flipped(total, bias[r // BLOCKS_PER_CHANNEL][:])
+            back = flip_back(total["bank"], D, RELU)
             result = results.tile([P, D], F32, name="result")
             nc.scalar.activation(result[:], back[:], COPY)
             nc.sync.dma_start(out[r * P : (r + 1) * P, :], result[:])
 
         r = BLOCKS - 1
         rows = out[r * P : (r + 1) * P, :]
-        left, right = open_sums(parts=2, terms=1 + K)
-        right["squares"] -= NEIGHBOURS_PER_PIECE * HALF // P
-        add_flipped([left, right], bias[r // BLOCKS_PER_CHANNEL], 0, D)
+        b_tile = bias[r // BLOCKS_PER_CHANNEL]
+        left = open_sum(HALF, 1 + K)
+        right = open_sum(HALF, (1 + K - NEIGHBOURS_PER_PIECE) * HALF_SQUARES)
+        add_plain(left, b_tile[:, 0:HALF])
+        add_flipped(right, b_tile[:, HALF:D])
         for m in range(PIECES - 1):
-            add_flipped([left, right], look_up(r, m * PIECE, PIECE), m * PIECE, PIECE)
-        for k in (K - 2, K - 1):
-            add_flipped([left, right], look_up(r, k * D, HALF), k * D, HALF)
-        right_prod = [look_up(r, k * D + HALF, HALF) for k in (K - 2, K - 1)]
-
+            prod = look_up(r, m * PIECE, PIECE)
+            for k in range(NEIGHBOURS_PER_PIECE):
+                add_flipped(right, prod[:, k * D + HALF : (k + 1) * D])
+            for k in range(NEIGHBOURS_PER_PIECE):
+                add_plain(left, prod[:, k * D : k * D + HALF])
         right_back = flip_back(right["bank"], HALF, COPY)
-        left_back = flip_back(left["bank"], HALF, RELU)
+
+        for k in (K - 2, K - 1):
+            add_plain(left, look_up(r, k * D, HALF)[:])
         left_result = results.tile([P, HALF], F32, name="left_result")
-        nc.scalar.activation(left_result[:], left_back[:], COPY)
+        nc.scalar.activation(left_result[:], left["bank"][:], RELU)
         nc.sync.dma_start(rows[:, 0:HALF], left_result[:])
 
-        all_but_last = results.tile([P, HALF], F32, name="all_but_last")
-        nc.vector.tensor_tensor(all_but_last[:], right_prod[0][:], right_back[:], ADD)
-        summed = results.tile([P, HALF], F32, name="summed")
-        nc.vector.tensor_tensor(summed[:], right_prod[1][:], all_but_last[:], ADD)
+        right_prod = [look_up(r, k * D + HALF, HALF) for k in (K - 2, K - 1)]
+        all_but_last = [results.tile([P, P], F32, name=f"all_but_last{s}") for s in range(HALF // P)]
+        summed = [results.tile([P, P], F32, name=f"summed{s}") for s in range(HALF // P)]
         right_result = results.tile([P, HALF], F32, name="right_result")
-        nc.vector.tensor_scalar_max(right_result[:], summed[:], 0.0)
+        squares = [slice(s * P, (s + 1) * P) for s in range(HALF // P)]
+        for s, square in enumerate(squares):
+            nc.vector.tensor_tensor(all_but_last[s][:], right_prod[0][:, square], right_back[:, square], ADD)
+        for s, square in enumerate(squares):
+            nc.vector.tensor_tensor(summed[s][:], right_prod[1][:, square], all_but_last[s][:], ADD)
+        for s, square in enumerate(squares):
+            nc.vector.tensor_scalar_max(right_result[:, square], summed[s][:], 0.0)
         nc.sync.dma_start(rows[:, HALF:D], right_result[:])

@@ -140,21 +140,23 @@ def tile_lcnchannelstack_kernel(tc, x, w, b, offs, out):
                 add_plain(left, prod[:, k * D : k * D + HALF])
         right_back = flip_back(right["bank"], HALF, COPY)
 
-        for k in (K - 2, K - 1):
-            add_plain(left, look_up(r, k * D, HALF)[:])
+        last_but_one = look_up(r, N - 2 * D, D)
+        add_plain(left, last_but_one[:, 0:HALF])
+        last_left = look_up(r, N - D, HALF)
+        add_plain(left, last_left[:])
         left_result = results.tile([P, HALF], F32, name="left_result")
         nc.scalar.activation(left_result[:], left["bank"][:], RELU)
         nc.sync.dma_start(rows[:, 0:HALF], left_result[:])
 
-        right_prod = [look_up(r, k * D + HALF, HALF) for k in (K - 2, K - 1)]
+        last_right = look_up(r, N - HALF, HALF)
         all_but_last = [results.tile([P, P], F32, name=f"all_but_last{s}") for s in range(HALF // P)]
         summed = [results.tile([P, P], F32, name=f"summed{s}") for s in range(HALF // P)]
         right_result = results.tile([P, HALF], F32, name="right_result")
         squares = [slice(s * P, (s + 1) * P) for s in range(HALF // P)]
         for s, square in enumerate(squares):
-            nc.vector.tensor_tensor(all_but_last[s][:], right_prod[0][:, square], right_back[:, square], ADD)
+            nc.vector.tensor_tensor(all_but_last[s][:], last_but_one[:, HALF + s * P : HALF + (s + 1) * P], right_back[:, square], ADD)
         for s, square in enumerate(squares):
-            nc.vector.tensor_tensor(summed[s][:], right_prod[1][:, square], all_but_last[s][:], ADD)
+            nc.vector.tensor_tensor(summed[s][:], last_right[:, square], all_but_last[s][:], ADD)
         for s, square in enumerate(squares):
             nc.vector.tensor_scalar_max(right_result[:, square], summed[s][:], 0.0)
         nc.sync.dma_start(rows[:, HALF:D], right_result[:])

@@ -90,8 +90,9 @@ def tile_lcnchannelstack_kernel(tc, x, w, b, offs, out):
                     **group_flags(group),
                 )
 
-        def add_plain(group, term):
-            nc.tensor.matmul(group["bank"][:], identity[:], term, **group_flags(group))
+        def add_plain(group, term, place=0):
+            columns = slice(place, place + term.shape[1])
+            nc.tensor.matmul(group["bank"][:, columns], identity[:], term, **group_flags(group))
 
         def flip_back(bank, columns, func):
             flipped = results.tile([P, columns], F32, name="flipped")
@@ -114,15 +115,16 @@ def tile_lcnchannelstack_kernel(tc, x, w, b, offs, out):
             return prod
 
         for r in range(BLOCKS - 1):
-            total = open_sum(D, (K + 1) * SQUARES)
-            cuts = FIRST_CUTS if r == 0 else [0, PIECE]
-            cuts = cuts + [m * PIECE for m in range(2, PIECES + 1)]
-            for lo, hi in zip(cuts[:-1], cuts[1:]):
-                add_flipped(total, look_up(r, lo, hi - lo)[:], lo // P)
-            add_flipped(total, bias[r // BLOCKS_PER_CHANNEL][:])
-            back = flip_back(total["bank"], D, RELU)
+            cuts = (FIRST_CUTS if r == 0 else [0, PIECE]) + [m * PIECE for m in range(2, PIECES + 1)]
+            parts = [(lo, hi, range(lo, hi, D)) for lo, hi in zip(cuts[:-1], cuts[1:])]
+            total = open_sum(D, 1 + sum(len(starts) for lo, hi, starts in parts))
+            for lo, hi, starts in parts:
+                prod = look_up(r, lo, hi - lo)
+                for start in starts:
+                    add_plain(total, prod[:, start - lo : min(start + D, hi) - lo], start % D)
+            add_plain(total, bias[r // BLOCKS_PER_CHANNEL][:])
             result = results.tile([P, D], F32, name="result")
-            nc.scalar.activation(result[:], back[:], COPY)
+            nc.scalar.activation(result[:], total["bank"][:], RELU)
             nc.sync.dma_start(out[r * P : (r + 1) * P, :], result[:])
 
         r = BLOCKS - 1

@@ -32,7 +32,7 @@ def tile_lcnchannelstack_kernel(tc, x, w, b, offs, out):
     nc = tc.nc
     with (
         tc.tile_pool(name="held", bufs=1) as held,
-        tc.tile_pool(name="products", bufs=4) as products,
+        tc.tile_pool(name="products", bufs=8) as products,
         tc.tile_pool(name="results", bufs=2) as results,
         tc.psum_pool(name="totals", bufs=3) as totals,
         tc.psum_pool(name="backs", bufs=2) as backs,

@@ -142,10 +142,9 @@ def tile_lcnchannelstack_kernel(tc, x, w, b, offs, out):
                 add_plain(left, prod[:, k * D : k * D + HALF])
         right_back = flip_back(right["bank"], HALF, COPY)
 
-        last_but_one = look_up(r, N - 2 * D, D)
-        add_plain(left, last_but_one[:, 0:HALF])
-        last_left = look_up(r, N - D, HALF)
-        add_plain(left, last_left[:])
+        first_run = look_up(r, N - 2 * D, D + HALF)
+        add_plain(left, first_run[:, 0:HALF])
+        add_plain(left, first_run[:, D : D + HALF])
         left_result = results.tile([P, HALF], F32, name="left_result")
         nc.scalar.activation(left_result[:], left["bank"][:], RELU)
         nc.sync.dma_start(rows[:, 0:HALF], left_result[:])
@@ -156,7 +155,7 @@ def tile_lcnchannelstack_kernel(tc, x, w, b, offs, out):
         right_result = results.tile([P, HALF], F32, name="right_result")
         squares = [slice(s * P, (s + 1) * P) for s in range(HALF // P)]
         for s, square in enumerate(squares):
-            nc.vector.tensor_tensor(all_but_last[s][:], last_but_one[:, HALF + s * P : HALF + (s + 1) * P], right_back[:, square], ADD)
+            nc.vector.tensor_tensor(all_but_last[s][:], first_run[:, HALF + s * P : HALF + (s + 1) * P], right_back[:, square], ADD)
         for s, square in enumerate(squares):
             nc.vector.tensor_tensor(summed[s][:], last_right[:, square], all_but_last[s][:], ADD)
         for s, square in enumerate(squares):

import concourse.mybir as mybir
from concourse.masks import make_identity

F32 = mybir.dt.float32
U16 = mybir.dt.uint16
MULT = mybir.AluOpType.mult
ADD = mybir.AluOpType.add
RELU = mybir.ActivationFunctionType.Relu
COPY = mybir.ActivationFunctionType.Copy

P = 128
CH = 2
ROWS = 512
S = 1024
D = 512
K = 8
N = K * D
BLOCKS = ROWS // P
BLOCKS_PER_CHANNEL = BLOCKS // CH
SQUARES = D // P
NEIGHBOURS_PER_PIECE = 2
PIECE = NEIGHBOURS_PER_PIECE * D
PIECES = N // PIECE
FIRST_CUTS = [0, 128, 512, 1024]
HALF = D // 2
HALF_SQUARES = HALF // P

FLOPS = 2 * ROWS * N


def tile_lcnchannelstack_kernel(tc, x, w, b, offs, out):
    nc = tc.nc
    with (
        tc.tile_pool(name="held", bufs=1) as held,
        tc.tile_pool(name="products", bufs=8) as products,
        tc.tile_pool(name="results", bufs=2) as results,
        tc.psum_pool(name="totals", bufs=3) as totals,
        tc.psum_pool(name="backs", bufs=2) as backs,
    ):
        identity = held.tile([P, P], F32, name="identity")
        make_identity(nc, identity[:])

        offsets = held.tile([P, N // 16], U16, name="offsets")
        x_block = [held.tile([P, S], F32, name=f"x{r}") for r in range(BLOCKS)]
        w_piece = [held.tile([P, PIECE], F32, name=f"w{i}") for i in range(CH * PIECES)]
        bias = [held.tile([P, D], F32, name=f"b{ch}") for ch in range(CH)]

        def load_x(r):
            nc.sync.dma_start(x_block[r][:], x[r * P : (r + 1) * P, :])

        def load_w(ch, m, lo=0, hi=PIECE):
            nc.sync.dma_start(
                w_piece[ch * PIECES + m][:, lo:hi], w[ch, m * PIECE + lo : m * PIECE + hi].partition_broadcast(P)
            )

        def load_b(ch):
            nc.sync.dma_start(bias[ch][:], b[ch, :].partition_broadcast(P))

        nc.sync.dma_start(offsets[:], offs)
        load_w(0, 0, FIRST_CUTS[0], FIRST_CUTS[1])
        load_x(0)
        for lo, hi in zip(FIRST_CUTS[1:-1], FIRST_CUTS[2:]):
            load_w(0, 0, lo, hi)
        for m in range(1, PIECES):
            load_w(0, m)
        load_b(0)
        load_x(1)
        load_x(2)
        for m in range(PIECES):
            load_w(1, m)
        load_b(1)
        load_x(3)

        def open_sum(columns, matmuls):
            return {"bank": totals.tile([P, columns], F32, name="total"), "done": 0, "matmuls": matmuls}

        def group_flags(group):
            group["done"] += 1
            return {"start": group["done"] == 1, "stop": group["done"] == group["matmuls"]}

        def add_flipped(group, term, first_square=0):
            squares = group["bank"][:].shape[1] // P
            for s in range(term.shape[1] // P):
                q = (first_square + s) % squares
                nc.tensor.matmul(
                    group["bank"][:, q * P : (q + 1) * P],
                    term[:, s * P : (s + 1) * P],
                    identity[:],
                    is_transpose=True,
                    **group_flags(group),
                )

        def add_plain(group, term, place=0):
            columns = slice(place, place + term.shape[1])
            nc.tensor.matmul(group["bank"][:, columns], identity[:], term, **group_flags(group))

        def flip_back(bank, columns, func):
            flipped = results.tile([P, columns], F32, name="flipped")
            nc.scalar.activation(flipped[:], bank[:], func)
            back = backs.tile([P, columns], F32, name="back")
            for q in range(columns // P):
                nc.tensor.transpose(back[:, q * P : (q + 1) * P], flipped[:, q * P : (q + 1) * P], identity[:])
            return back

        def look_up(r, first_entry, entries):
            ch = r // BLOCKS_PER_CHANNEL
            m, start = divmod(first_entry, PIECE)
            prod = products.tile([P, entries], F32, name="prod")
            nc.vector.tensor_tensor(
                prod[:],
                x_block[r][:].indirect(offsets[:, first_entry // 16 : (first_entry + entries) // 16]),
                w_piece[ch * PIECES + m][:, start : start + entries],
                MULT,
            )
            return prod

        for r in range(BLOCKS - 1):
            cuts = (FIRST_CUTS if r == 0 else [0, PIECE]) + [m * PIECE for m in range(2, PIECES + 1)]
            parts = [(lo, hi, range(lo, hi, D)) for lo, hi in zip(cuts[:-1], cuts[1:])]
            total = open_sum(D, 1 + sum(len(starts) for lo, hi, starts in parts))
            for lo, hi, starts in parts:
                prod = look_up(r, lo, hi - lo)
                for start in starts:
                    add_plain(total, prod[:, start - lo : min(start + D, hi) - lo], start % D)
            add_plain(total, bias[r // BLOCKS_PER_CHANNEL][:])
            result = results.tile([P, D], F32, name="result")
            nc.scalar.activation(result[:], total["bank"][:], RELU)
            nc.sync.dma_start(out[r * P : (r + 1) * P, :], result[:])

        r = BLOCKS - 1
        rows = out[r * P : (r + 1) * P, :]
        b_tile = bias[r // BLOCKS_PER_CHANNEL]
        left = open_sum(HALF, 1 + K)
        right = open_sum(HALF, (1 + K - NEIGHBOURS_PER_PIECE) * HALF_SQUARES)
        add_plain(left, b_tile[:, 0:HALF])
        add_flipped(right, b_tile[:, HALF:D])
        for m in range(PIECES - 1):
            prod = look_up(r, m * PIECE, PIECE)
            for k in range(NEIGHBOURS_PER_PIECE):
                add_flipped(right, prod[:, k * D + HALF : (k + 1) * D])
            for k in range(NEIGHBOURS_PER_PIECE):
                add_plain(left, prod[:, k * D : k * D + HALF])
        right_back = flip_back(right["bank"], HALF, COPY)

        first_run = look_up(r, N - 2 * D, D + HALF)
        add_plain(left, first_run[:, 0:HALF])
        add_plain(left, first_run[:, D : D + HALF])
        left_result = results.tile([P, HALF], F32, name="left_result")
        nc.scalar.activation(left_result[:], left["bank"][:], RELU)
        nc.sync.dma_start(rows[:, 0:HALF], left_result[:])

        last_right = look_up(r, N - HALF, HALF)
        all_but_last = [results.tile([P, P], F32, name=f"all_but_last{s}") for s in range(HALF // P)]
        summed = [results.tile([P, P], F32, name=f"summed{s}") for s in range(HALF // P)]
        right_result = results.tile([P, HALF], F32, name="right_result")
        squares = [slice(s * P, (s + 1) * P) for s in range(HALF // P)]
        for s, square in enumerate(squares):
            nc.vector.tensor_tensor(all_but_last[s][:], first_run[:, HALF + s * P : HALF + (s + 1) * P], right_back[:, square], ADD)
        for s, square in enumerate(squares):
            nc.vector.tensor_tensor(summed[s][:], last_right[:, square], all_but_last[s][:], ADD)
        for s, square in enumerate(squares):
            nc.vector.tensor_scalar_max(right_result[:, square], summed[s][:], 0.0)
        nc.sync.dma_start(rows[:, HALF:D], right_result[:])
